import numpy as np
import ml_dtypes


def mxq(x, axis, fmt="e4m3"):
    dtype, down = {"e4m3": (ml_dtypes.float8_e4m3fn, 7), "e5m2": (ml_dtypes.float8_e5m2, 14)}[fmt]
    v = np.moveaxis(np.asarray(x, np.float32).astype(ml_dtypes.bfloat16).astype(np.float64), axis, -1)
    blocks = v.reshape(v.shape[:-1] + (-1, 32))
    amax = np.abs(blocks).max(-1, keepdims=True)
    byte = np.maximum(np.where(amax > 0, np.frexp(amax)[1] - 1 + 127, 0) - down, 1)
    scale = np.exp2(byte - 127.0)
    codes = (blocks / scale).astype(np.float32).astype(dtype).astype(np.float64)
    return np.moveaxis((codes * scale).reshape(v.shape), -1, axis)


WIDE = False


def mx_kscale(k):
    if not WIDE:
        return np.ones(k)
    levels = np.array([10, -10, 5, -5, 0])
    if k % 512:
        return np.exp2(np.random.permutation(np.resize(levels, k // 32))).repeat(32)
    a = np.empty((k // 512, 16))
    for p in range(k // 512):
        a[p, :8] = np.random.permutation(np.resize(levels, 8))
        for g in range(8):
            far = levels[np.abs(levels - a[p, g]) >= 10]
            a[p, g + 8] = far[np.random.randint(len(far))]
    return np.exp2(a.ravel()).repeat(32)


BF16 = ml_dtypes.bfloat16


def bf(x):
    return np.asarray(x, np.float32).astype(BF16)


def f64(x):
    return np.asarray(x).astype(np.float64)


B, IN, L = 256, 2048, 1536


def sigmoid(v):
    return 1.0 / (1.0 + np.exp(-v))


def setup_inputs():
    s = mx_kscale(IN)
    return {"input": bf(np.random.standard_normal((B, IN)) * s),
            "h0": bf(np.random.standard_normal((B, L))),
            "gh0": bf(np.random.standard_normal((B, 3 * L)) * 0.75),
            "W_ih0": bf(np.random.standard_normal((3 * L, IN)) * 0.7 / np.sqrt(IN) / s),
            "b_ih0": bf(np.random.standard_normal(3 * L) * 0.3)}


def core(input, h0, gh0, W_ih0, b_ih0):
    h, gh = f64(h0), f64(gh0)
    gi = (mxq(f64(input), 1, "e4m3") @ mxq(f64(W_ih0), 1, "e4m3").T) + f64(b_ih0)
    i_r, i_z, i_n = gi[:, :L], gi[:, L:2 * L], gi[:, 2 * L:]
    h_r, h_z, h_n = gh[:, :L], gh[:, L:2 * L], gh[:, 2 * L:]
    r = sigmoid(i_r + h_r)
    z = sigmoid(i_z + h_z)
    n = np.tanh(i_n + r * h_n)
    return (1.0 - z) * n + z * h


def e4m3fn_bytes(y):
    return np.clip(np.asarray(y, np.float64), -448.0, 448.0).astype(np.float32).astype(ml_dtypes.float8_e4m3fn).view(np.uint8)


def reference(input, h0, gh0, W_ih0, b_ih0):
    out = core(input, h0, gh0, W_ih0, b_ih0)
    s = np.max(np.abs(out), axis=-1, keepdims=True) / 448.0
    return out, e4m3fn_bytes(out / s)

@@ -1,0 +1,371 @@
+from contextlib import ExitStack
+
+import concourse.mybir as mybir
+from concourse.masks import make_identity
+
+F32 = mybir.dt.float32
+BF16 = mybir.dt.bfloat16
+U32 = mybir.dt.uint32
+U8 = mybir.dt.uint8
+FP8X4 = mybir.dt.float8_e4m3fn_x4
+FP8 = mybir.dt.float8_e4m3fn
+ALU = mybir.AluOpType
+ACT = mybir.ActivationFunctionType
+AX = mybir.AxisListType
+
+B, IN, L = 256, 2048, 1536
+FLOPS = 2 * B * IN * 3 * L
+
+P = 128
+CW = 256
+NCH = L // CW
+HALF_UNITS = 3
+RAW_FULL = 6
+STORE_FROM = 3
+GR, GZ, GN = 0, 1, 2
+
+
+def tile_grucellstack_pa_kernel(tc, x, h0, gh0, w, b, out_0, out_1):
+    nc = tc.nc
+    with ExitStack() as ctx:
+        const = ctx.enter_context(tc.tile_pool(name="const", bufs=1))
+        rawp = ctx.enter_context(tc.tile_pool(name="rawp", bufs=RAW_FULL))
+        grp = ctx.enter_context(tc.tile_pool(name="grp", bufs=3))
+        cdp = ctx.enter_context(tc.tile_pool(name="cdp", bufs=3))
+        wk = ctx.enter_context(tc.tile_pool(name="wk", bufs=2))
+        tps = ctx.enter_context(tc.psum_pool(name="tps", bufs=5))
+        accs = ctx.enter_context(tc.psum_pool(name="accs", bufs=3))
+        ctx.enter_context(tc.manual_schedule())
+
+        units = [(x, 0, 2)]
+        for c in range(NCH):
+            units.append((w, GR * L + c * CW, 2))
+            units.append((w, GN * L + c * CW, 2))
+            if c < NCH - 1:
+                units.append((w, GZ * L + c * CW, 2))
+            else:
+                units.append((w, GZ * L + c * CW, 1))
+                units.append((w, GZ * L + c * CW + P, 1))
+        n_units = len(units)
+
+        btile = const.tile([P, 512], BF16, name="btile")
+        nc.vector.memset(btile[:], 0.0)
+        ztile = const.tile([P, 512], BF16, name="ztile")
+        nc.vector.memset(ztile[:], 0.0)
+        zeros = const.tile([P, 1], F32, name="zeros")
+        nc.vector.memset(zeros[:], 0.0)
+        ident_b = const.tile([P, P], BF16, name="ident_b")
+        make_identity(nc, ident_b[:])
+        ident_f = const.tile([P, P], F32, name="ident_f")
+        make_identity(nc, ident_f[:])
+        scr = const.tile([P, 1], F32, name="scr")
+        nc.scalar.activation(out=scr[:], in_=zeros[:], func=ACT.Sigmoid)
+
+        bias_bc = const.tile([P, 3 * L], BF16, name="bias_bc")
+        xcodes = const.tile([P, 4, CW], U32, name="xcodes", align_bytes=64)
+        xscales = const.tile([P, 4, CW], U8, name="xscales", align_bytes=64)
+        o_all = const.tile([P, 2, L + 8], F32, name="o_all")
+        q_all = const.tile([P, 2, L], FP8, name="q_all")
+        stats = const.tile([P, 2, 8], F32, name="stats")
+
+        raw = {}
+        grouped = {}
+        codes = {0: xcodes}
+        scales = {0: xscales}
+        acc = {}
+        ghp = {}
+        hp = {}
+        gsum = {}
+        t = {}
+
+        def load_gh(gate, cc):
+            g_t = const.tile([P, 2, 512], BF16, name="gh%d_%d" % (gate, cc))
+            lo = gate * L + cc * 512
+            nc.sync.dma_start(out=g_t[:], in_=gh0[:, lo : lo + 512].rearrange("(m p) n -> p m n", p=P))
+            ghp[(gate, cc)] = g_t
+
+        def load_h(cc):
+            h_t = const.tile([P, 2, 512], BF16, name="h_%d" % cc)
+            nc.sync.dma_start(
+                out=h_t[:], in_=h0[:, cc * 512 : (cc + 1) * 512].rearrange("(m p) n -> p m n", p=P)
+            )
+            hp[cc] = h_t
+
+        extras = {}
+        for cc in range(3):
+            extras[2 + 3 * cc] = [(GR, cc)]
+            extras[3 + 3 * cc] = [(GN, cc)]
+            extras[4 + 3 * cc] = [(GZ, cc), (3, cc)]
+
+        def issue_load(k):
+            if k >= n_units:
+                return
+            src, r0, nj = units[k]
+            halves = []
+            if k < HALF_UNITS:
+                for hf in range(2):
+                    r_t = rawp.tile([P, nj, 1024], BF16, name="rawh", tag="rawh", bufs=2 * HALF_UNITS)
+                    nc.sync.dma_start(
+                        out=r_t[:],
+                        in_=src[r0 : r0 + nj * P, hf * 1024 : (hf + 1) * 1024].rearrange("(j p) k -> p j k", p=P),
+                    )
+                    halves.append(r_t)
+                    if k == 0 and hf == 0:
+                        nc.sync.dma_start(out=btile[0:9, :], in_=b.rearrange("(q n) -> q n", q=9))
+            else:
+                r_t = rawp.tile([P, nj, IN], BF16, name="rawf", tag="rawf", bufs=RAW_FULL)
+                nc.sync.dma_start(out=r_t[:], in_=src[r0 : r0 + nj * P, :].rearrange("(j p) k -> p j k", p=P))
+                halves = [r_t[:, :, 0:1024], r_t[:, :, 1024:IN]]
+            raw[k] = halves
+            for gate, cc in extras.get(k, []):
+                if gate == 3:
+                    load_h(cc)
+                else:
+                    load_gh(gate, cc)
+
+        def transposes(k, first, count):
+            nj = units[k][2]
+            if first == 0:
+                grouped[k] = grp.tile([P, 4, nj * P, 4], BF16, name="grouped", tag="grouped", align_bytes=64)
+            for bq in range(first, first + count):
+                bank = tps.tile([P, 2, 2, P], F32, name="tp", tag="tp")
+                for s in range(2):
+                    if nj == 2:
+                        g, j = bq, s
+                    else:
+                        g, j = 2 * bq + s, 0
+                    hf, gl = divmod(g, 2)
+                    words = raw[k][hf][:, j, :].bitcast(F32)
+                    for u in range(2):
+                        nc.tensor.transpose(
+                            bank[:, s, u, :], words[:, 256 * gl + u : 256 * (gl + 1) : 2], ident_f[:]
+                        )
+                if nj == 2:
+                    dst = grouped[k][:, bq, :, :].bitcast(F32).rearrange("p (s r) u -> p s r u", s=2)
+                else:
+                    dst = grouped[k][:, 2 * bq : 2 * bq + 2, :, :].bitcast(F32)
+                nc.scalar.copy(out=dst, in_=bank[:].rearrange("p s u r -> p s r u"))
+
+        def quantize(k, parts=1):
+            nj = units[k][2]
+            if k > 0:
+                codes[k] = cdp.tile([P, 4, nj * P], U32, name="wc", tag="wc", align_bytes=64)
+                scales[k] = cdp.tile([P, 4, nj * P], U8, name="ws", tag="ws", align_bytes=64)
+            ng = 4 // parts
+            for g0 in range(0, 4, ng):
+                nc.vector.quantize_mx(
+                    out=codes[k][:, g0 : g0 + ng, :].rearrange("p g c -> p (g c)").bitcast(FP8X4),
+                    scales=scales[k][:, g0 : g0 + ng, :].rearrange("p g c -> p (g c)"),
+                    in_=grouped[k][:, g0 : g0 + ng, :, :].rearrange("p g c t -> p (g c t)"),
+                )
+
+        def matmuls(k):
+            nj = units[k][2]
+            a_t = accs.tile([P, 2, nj * P], F32, name="acc", tag="acc")
+            for m in range(2):
+                for g in range(4):
+                    nc.tensor.matmul_mx(
+                        out=a_t[:, m, :],
+                        lhsT=xcodes[:, g, m * P : (m + 1) * P].bitcast(FP8X4),
+                        lhsT_scale=xscales[:, g, m * P : (m + 1) * P],
+                        rhs=codes[k][:, g, :].bitcast(FP8X4),
+                        rhs_scale=scales[k][:, g, :],
+                        start=(g == 0),
+                        stop=(g == 3),
+                    )
+            acc[k] = a_t
+
+        def warm_mm(count):
+            ps = accs.tile([P, 512], F32, name="wps", tag="acc")
+            for rep in range(count):
+                nc.tensor.matmul(out=ps[:], lhsT=ident_b[:], rhs=ztile[:], start=True, stop=True)
+
+        def bias_mm(q):
+            ps = accs.tile([P, 512], F32, name="bps", tag="acc")
+            nc.tensor.matmul(
+                out=ps[:], lhsT=ident_b[:, q : q + 1].to_broadcast([P, P]), rhs=btile[:], start=True, stop=True
+            )
+            nc.vector.tensor_copy(out=bias_bc[:, 512 * q : 512 * (q + 1)], in_=ps[:])
+
+        def work(name, wd):
+            return wk.tile([P, 2, wd], F32, name=name, tag=name)
+
+        def tt(out, in0, in1, op):
+            nc.vector.tensor_tensor(out=out, in0=in0, in1=in1, op=op)
+
+        def part(tile_ap, c, lo, wd):
+            off = (c % 2) * CW + lo
+            return tile_ap[:, :, off : off + wd]
+
+        def g_sum(gate, cc):
+            gsum[(gate, cc)] = const.tile([P, 2, 512], F32, name="gs%d_%d" % (gate, cc))
+            lo = gate * L + cc * 512
+            tt(
+                gsum[(gate, cc)][:],
+                ghp[(gate, cc)][:],
+                bias_bc[:, lo : lo + 512].unsqueeze(1).to_broadcast([P, 2, 512]),
+                ALU.add,
+            )
+
+        def a_rz(gate, k, c, lo, wd):
+            t[("A", gate, c, lo)] = work("A%d" % gate, wd)
+            tt(t[("A", gate, c, lo)][:], acc[k][:], part(gsum[(gate, c // 2)], c, lo, wd), ALU.add)
+
+        def act(dst, src, key, func, wd):
+            t[key] = src
+            nc.scalar.activation(out=src[:], in_=src[:], func=func)
+
+        def a_n(k, c):
+            t[("A", GN, c)] = work("A2", CW)
+            lo = GN * L + c * CW
+            tt(
+                t[("A", GN, c)][:],
+                acc[k][:],
+                bias_bc[:, lo : lo + CW].unsqueeze(1).to_broadcast([P, 2, CW]),
+                ALU.add,
+            )
+
+        def u_mul(c):
+            t[("u", c)] = work("u", CW)
+            tt(t[("u", c)][:], t[("r", c)][:], part(ghp[(GN, c // 2)], c, 0, CW), ALU.mult)
+
+        def v_add(c):
+            t[("v", c)] = work("v", CW)
+            tt(t[("v", c)][:], t[("A", GN, c)][:], t[("u", c)][:], ALU.add)
+
+        def d_sub(c):
+            t[("d", c)] = work("d", CW)
+            tt(t[("d", c)][:], part(hp[c // 2], c, 0, CW), t[("n", c)][:], ALU.subtract)
+
+        def e_mul(c, lo, wd):
+            t[("e", c, lo)] = work("e", wd)
+            tt(t[("e", c, lo)][:], t[("z", c, lo)][:], t[("d", c)][:, :, lo : lo + wd], ALU.mult)
+
+        def o_add(c, lo, wd):
+            cols = slice(c * CW + lo, c * CW + lo + wd)
+            tt(o_all[:, :, cols], t[("n", c)][:, :, lo : lo + wd], t[("e", c, lo)][:], ALU.add)
+            if c == STORE_FROM:
+                cols = slice(0, (c + 1) * CW)
+            if c >= STORE_FROM:
+                nc.sync.dma_start(out=out_0[:, cols].rearrange("(m p) n -> p m n", p=P), in_=o_all[:, :, cols])
+
+        def amax(dst, m, lo, hi):
+            nc.vector.tensor_reduce(
+                out=dst, in_=o_all[:, m, lo:hi], axis=AX.X, op=ALU.max, apply_absolute_value=True
+            )
+
+        def amax_chunk(c, m):
+            amax(stats[:, m, c : c + 1], m, c * CW, (c + 1) * CW)
+
+        for k in range(HALF_UNITS + RAW_FULL):
+            issue_load(k)
+        warm_mm(3)
+        early_gsum = {2: (GR, 0), 3: (GZ, 0), 5: (GR, 1), 8: (GZ, 1), 11: (GR, 2), 14: (GZ, 2)}
+        last = NCH - 1
+
+        for p in range(n_units + 1):
+            if p < n_units:
+                n_banks = 2 * units[p][2]
+                if p == 0:
+                    transposes(p, 0, 2)
+                    bias_mm(0)
+                    bias_mm(3)
+                    transposes(p, 2, 2)
+                    bias_mm(6)
+                    bias_mm(1)
+                else:
+                    transposes(p, 0, n_banks)
+                if p == 1:
+                    bias_mm(4)
+                    bias_mm(7)
+                if p == 2:
+                    bias_mm(2)
+                    bias_mm(5)
+                if p == 3:
+                    bias_mm(8)
+                if p >= HALF_UNITS:
+                    issue_load(p + RAW_FULL)
+            if p >= 2:
+                matmuls(p - 1)
+            if p >= 3:
+                c, ph = divmod(p - 3, 3)
+                k0 = 1 + 3 * c
+                if ph == 0:
+                    if c >= 1:
+                        e_mul(c - 1, 0, CW)
+                    a_rz(GR, k0, c, 0, CW)
+                    if c >= 1:
+                        o_add(c - 1, 0, CW)
+                    act("r", t[("A", GR, c, 0)], ("r", c), ACT.Sigmoid, CW)
+                elif ph == 1:
+                    a_n(k0 + 1, c)
+                    u_mul(c)
+                    if c == last:
+                        amax_chunk(c - 1, 0)
+                        amax_chunk(c - 1, 1)
+                        quantize(p, 2)
+                    elif c >= 1:
+                        amax_chunk(c - 1, 0)
+                    v_add(c)
+                    act("n", t[("v", c)], ("n", c), ACT.Tanh, CW)
+                elif c < last:
+                    d_sub(c)
+                    a_rz(GZ, k0 + 2, c, 0, CW)
+                    act("z", t[("A", GZ, c, 0)], ("z", c, 0), ACT.Sigmoid, CW)
+                    if c >= 1:
+                        amax_chunk(c - 1, 1)
+            if p in early_gsum:
+                g_sum(early_gsum[p][0], early_gsum[p][1])
+            if p < n_units - 1:
+                quantize(p)
+
+        c = last
+        k0 = 1 + 3 * c
+        a_rz(GZ, k0 + 2, c, 0, P)
+        act("z", t[("A", GZ, c, 0)], ("z", c, 0), ACT.Sigmoid, P)
+        nc.vector.tensor_reduce(out=o_all[:, :, L : L + 1], in_=stats[:, :, 0:last], axis=AX.X, op=ALU.max)
+        d_sub(c)
+        a_rz(GZ, k0 + 3, c, P, P)
+        act("z", t[("A", GZ, c, P)], ("z", c, P), ACT.Sigmoid, P)
+        e_mul(c, 0, P)
+        o_add(c, 0, P)
+        t[("e", c, P)] = work("e", P)
+        cols = slice(L - P, L)
+        for m in range(2):
+            tt(t[("e", c, P)][:, m, :], t[("z", c, P)][:, m, :], t[("d", c)][:, m, P:CW], ALU.mult)
+        for m in range(2):
+            tt(o_all[:, m, cols], t[("n", c)][:, m, P:CW], t[("e", c, P)][:, m, :], ALU.add)
+        nc.sync.dma_start(out=out_0[:, cols].rearrange("(m p) n -> p m n", p=P), in_=o_all[:, :, cols])
+
+        amx = const.tile([P, 2], F32, name="amx")
+        rcp = const.tile([P, 2], F32, name="rcp")
+        fac = const.tile([P, 2], F32, name="fac")
+        for m in (0, 1):
+            amax(amx[:, m : m + 1], m, L - CW, L + 1)
+        for m in (0, 1):
+            nc.vector.reciprocal(out=rcp[:, m : m + 1], in_=amx[:, m : m + 1])
+        for m in (1, 0):
+            nc.vector.tensor_scalar(
+                out=fac[:, m : m + 1], in0=rcp[:, m : m + 1], scalar1=448.0, scalar2=None, op0=ALU.mult
+            )
+        nc.scalar.activation(
+            out=q_all[:, 1, 512:L],
+            in_=o_all[:, 1, 512:L],
+            func=ACT.Identity,
+            scale=fac[:, 1:2],
+            bias=zeros[:, 0:1],
+            saturate=False,
+        )
+        nc.vector.tensor_scalar(
+            out=q_all[:, 0, :], in0=o_all[:, 0, 0:L], scalar1=fac[:, 0:1], scalar2=None, op0=ALU.mult, saturate=False
+        )
+        nc.sync.dma_start(out=out_1[0:P, :], in_=q_all[:, 0, :].bitcast(U8))
+        nc.vector.tensor_scalar(
+            out=q_all[:, 1, 0:512],
+            in0=o_all[:, 1, 0:512],
+            scalar1=fac[:, 1:2],
+            scalar2=None,
+            op0=ALU.mult,
+            saturate=False,
+        )
+        nc.sync.dma_start(out=out_1[P : 2 * P, :], in_=q_all[:, 1, :].bitcast(U8))

@@ -263,7 +263,7 @@ def tile_grucellstack_pa_kernel(tc, x, h0, gh0, w, b, out_0, out_1):
         early_gsum = {2: (GR, 0), 3: (GZ, 0), 5: (GR, 1), 8: (GZ, 1), 11: (GR, 2), 14: (GZ, 2)}
         last = NCH - 1
 
-        for p in range(n_units + 1):
+        for p in range(n_units - 3):
             if p < n_units:
                 n_banks = 2 * units[p][2]
                 if p == 0:
@@ -321,20 +321,50 @@ def tile_grucellstack_pa_kernel(tc, x, h0, gh0, w, b, out_0, out_1):
 
         c = last
         k0 = 1 + 3 * c
-        a_rz(GZ, k0 + 2, c, 0, P)
+        ka, kb = k0 + 2, k0 + 3
+        transposes(k0 + 1, 0, 4)
+        matmuls(k0)
+        d_sub(c - 1)
+        a_rz(GZ, k0 - 1, c - 1, 0, CW)
+        act("z", t[("A", GZ, c - 1, 0)], ("z", c - 1, 0), ACT.Sigmoid, CW)
+        amax_chunk(c - 2, 1)
+        quantize(k0 + 1)
+        transposes(ka, 0, 1)
+        a_rz(GR, k0, c, 0, CW)
+        act("r", t[("A", GR, c, 0)], ("r", c), ACT.Sigmoid, CW)
+        transposes(ka, 1, 1)
+        matmuls(k0 + 1)
+        e_mul(c - 1, 0, CW)
+        o_add(c - 1, 0, CW)
+        u_mul(c)
+        transposes(kb, 0, 2)
+        a_n(k0 + 1, c)
+        quantize(ka)
+        matmuls(ka)
+        v_add(c)
+        act("n", t[("v", c)], ("n", c), ACT.Tanh, CW)
+        t[("d", c)] = work("d", CW)
+        nc.gpsimd.tensor_tensor(
+            out=t[("d", c)][:], in0=part(hp[c // 2], c, 0, CW), in1=t[("n", c)][:], op=ALU.subtract
+        )
+        quantize(kb)
+        matmuls(kb)
+        a_rz(GZ, ka, c, 0, P)
         act("z", t[("A", GZ, c, 0)], ("z", c, 0), ACT.Sigmoid, P)
-        nc.vector.tensor_reduce(out=o_all[:, :, L : L + 1], in_=stats[:, :, 0:last], axis=AX.X, op=ALU.max)
-        d_sub(c)
-        a_rz(GZ, k0 + 3, c, P, P)
+        amax_chunk(c - 1, 0)
+        amax_chunk(c - 1, 1)
+        a_rz(GZ, kb, c, P, P)
         act("z", t[("A", GZ, c, P)], ("z", c, P), ACT.Sigmoid, P)
+        nc.vector.tensor_reduce(out=o_all[:, :, L : L + 1], in_=stats[:, :, 0:last], axis=AX.X, op=ALU.max)
         e_mul(c, 0, P)
-        o_add(c, 0, P)
         t[("e", c, P)] = work("e", P)
         cols = slice(L - P, L)
         for m in range(2):
             tt(t[("e", c, P)][:, m, :], t[("z", c, P)][:, m, :], t[("d", c)][:, m, P:CW], ALU.mult)
+        tt(o_all[:, :, L - CW : L - P], t[("n", c)][:, :, 0:P], t[("e", c, 0)][:], ALU.add)
         for m in range(2):
             tt(o_all[:, m, cols], t[("n", c)][:, m, P:CW], t[("e", c, P)][:, m, :], ALU.add)
+        cols = slice(L - CW, L)
         nc.sync.dma_start(out=out_0[:, cols].rearrange("(m p) n -> p m n", p=P), in_=o_all[:, :, cols])
 
         amx = const.tile([P, 2], F32, name="amx")

@@ -328,11 +328,10 @@ def tile_grucellstack_pa_kernel(tc, x, h0, gh0, w, b, out_0, out_1):
         a_rz(GZ, k0 - 1, c - 1, 0, CW)
         act("z", t[("A", GZ, c - 1, 0)], ("z", c - 1, 0), ACT.Sigmoid, CW)
         amax_chunk(c - 2, 1)
-        quantize(k0 + 1)
-        transposes(ka, 0, 1)
+        quantize(k0 + 1, 2)
         a_rz(GR, k0, c, 0, CW)
         act("r", t[("A", GR, c, 0)], ("r", c), ACT.Sigmoid, CW)
-        transposes(ka, 1, 1)
+        transposes(ka, 0, 2)
         matmuls(k0 + 1)
         e_mul(c - 1, 0, CW)
         o_add(c - 1, 0, CW)
@@ -347,13 +346,28 @@ def tile_grucellstack_pa_kernel(tc, x, h0, gh0, w, b, out_0, out_1):
         nc.gpsimd.tensor_tensor(
             out=t[("d", c)][:], in0=part(hp[c // 2], c, 0, CW), in1=t[("n", c)][:], op=ALU.subtract
         )
-        quantize(kb)
-        matmuls(kb)
+        quantize(kb, 2)
+        acc_m = []
+        for m in range(2):
+            acc_m.append(accs.tile([P, P], F32, name="accm", tag="acc"))
+        for g in range(4):
+            for m in range(2):
+                nc.tensor.matmul_mx(
+                    out=acc_m[m][:],
+                    lhsT=xcodes[:, g, m * P : (m + 1) * P].bitcast(FP8X4),
+                    lhsT_scale=xscales[:, g, m * P : (m + 1) * P],
+                    rhs=codes[kb][:, g, :].bitcast(FP8X4),
+                    rhs_scale=scales[kb][:, g, :],
+                    start=(g == 0),
+                    stop=(g == 3),
+                )
         a_rz(GZ, ka, c, 0, P)
         act("z", t[("A", GZ, c, 0)], ("z", c, 0), ACT.Sigmoid, P)
         amax_chunk(c - 1, 0)
         amax_chunk(c - 1, 1)
-        a_rz(GZ, kb, c, P, P)
+        t[("A", GZ, c, P)] = work("A1", P)
+        for m in range(2):
+            tt(t[("A", GZ, c, P)][:, m, :], acc_m[m][:], part(gsum[(GZ, c // 2)], c, P, P)[:, m, :], ALU.add)
         act("z", t[("A", GZ, c, P)], ("z", c, P), ACT.Sigmoid, P)
         nc.vector.tensor_reduce(out=o_all[:, :, L : L + 1], in_=stats[:, :, 0:last], axis=AX.X, op=ALU.max)
         e_mul(c, 0, P)
@@ -390,6 +404,7 @@ def tile_grucellstack_pa_kernel(tc, x, h0, gh0, w, b, out_0, out_1):
             out=q_all[:, 0, :], in0=o_all[:, 0, 0:L], scalar1=fac[:, 0:1], scalar2=None, op0=ALU.mult, saturate=False
         )
         nc.sync.dma_start(out=out_1[0:P, :], in_=q_all[:, 0, :].bitcast(U8))
+        nc.sync.dma_start(out=out_1[P : 2 * P, 512:L], in_=q_all[:, 1, 512:L].bitcast(U8))
         nc.vector.tensor_scalar(
             out=q_all[:, 1, 0:512],
             in0=o_all[:, 1, 0:512],
@@ -398,4 +413,4 @@ def tile_grucellstack_pa_kernel(tc, x, h0, gh0, w, b, out_0, out_1):
             op0=ALU.mult,
             saturate=False,
         )
-        nc.sync.dma_start(out=out_1[P : 2 * P, :], in_=q_all[:, 1, :].bitcast(U8))
+        nc.sync.dma_start(out=out_1[P : 2 * P, 0:512], in_=q_all[:, 1, 0:512].bitcast(U8))

@@ -22,6 +22,7 @@ NCH = L // CW
 HALF_UNITS = 3
 RAW_FULL = 6
 STORE_FROM = 3
+SPLIT = 640
 GR, GZ, GN = 0, 1, 2
 
 
@@ -333,8 +334,13 @@ def tile_grucellstack_pa_kernel(tc, x, h0, gh0, w, b, out_0, out_1):
         act("r", t[("A", GR, c, 0)], ("r", c), ACT.Sigmoid, CW)
         transposes(ka, 0, 2)
         matmuls(k0 + 1)
-        e_mul(c - 1, 0, CW)
-        o_add(c - 1, 0, CW)
+        t[("e", c - 1, 0)] = work("e", CW)
+        cols = slice((c - 1) * CW, c * CW)
+        for m in range(2):
+            tt(t[("e", c - 1, 0)][:, m, :], t[("z", c - 1, 0)][:, m, :], t[("d", c - 1)][:, m, :], ALU.mult)
+        for m in range(2):
+            tt(o_all[:, m, cols], t[("n", c - 1)][:, m, :], t[("e", c - 1, 0)][:, m, :], ALU.add)
+        nc.sync.dma_start(out=out_0[:, cols].rearrange("(m p) n -> p m n", p=P), in_=o_all[:, :, cols])
         u_mul(c)
         transposes(kb, 0, 2)
         a_n(k0 + 1, c)
@@ -388,13 +394,13 @@ def tile_grucellstack_pa_kernel(tc, x, h0, gh0, w, b, out_0, out_1):
             amax(amx[:, m : m + 1], m, L - CW, L + 1)
         for m in (0, 1):
             nc.vector.reciprocal(out=rcp[:, m : m + 1], in_=amx[:, m : m + 1])
-        for m in (1, 0):
+        for m in (0, 1):
             nc.vector.tensor_scalar(
                 out=fac[:, m : m + 1], in0=rcp[:, m : m + 1], scalar1=448.0, scalar2=None, op0=ALU.mult
             )
         nc.scalar.activation(
-            out=q_all[:, 1, 512:L],
-            in_=o_all[:, 1, 512:L],
+            out=q_all[:, 1, SPLIT:L],
+            in_=o_all[:, 1, SPLIT:L],
             func=ACT.Identity,
             scale=fac[:, 1:2],
             bias=zeros[:, 0:1],
@@ -404,13 +410,13 @@ def tile_grucellstack_pa_kernel(tc, x, h0, gh0, w, b, out_0, out_1):
             out=q_all[:, 0, :], in0=o_all[:, 0, 0:L], scalar1=fac[:, 0:1], scalar2=None, op0=ALU.mult, saturate=False
         )
         nc.sync.dma_start(out=out_1[0:P, :], in_=q_all[:, 0, :].bitcast(U8))
-        nc.sync.dma_start(out=out_1[P : 2 * P, 512:L], in_=q_all[:, 1, 512:L].bitcast(U8))
+        nc.sync.dma_start(out=out_1[P : 2 * P, SPLIT:L], in_=q_all[:, 1, SPLIT:L].bitcast(U8))
         nc.vector.tensor_scalar(
-            out=q_all[:, 1, 0:512],
-            in0=o_all[:, 1, 0:512],
+            out=q_all[:, 1, 0:SPLIT],
+            in0=o_all[:, 1, 0:SPLIT],
             scalar1=fac[:, 1:2],
             scalar2=None,
             op0=ALU.mult,
             saturate=False,
         )
-        nc.sync.dma_start(out=out_1[P : 2 * P, 0:512], in_=q_all[:, 1, 0:512].bitcast(U8))
+        nc.sync.dma_start(out=out_1[P : 2 * P, 0:SPLIT], in_=q_all[:, 1, 0:SPLIT].bitcast(U8))

@@ -92,11 +92,18 @@ def tile_grucellstack_pa_kernel(tc, x, h0, gh0, w, b, out_0, out_1):
             )
             hp[cc] = h_t
 
-        extras = {}
-        for cc in range(3):
-            extras[2 + 3 * cc] = [(GR, cc)]
-            extras[3 + 3 * cc] = [(GN, cc)]
-            extras[4 + 3 * cc] = [(GZ, cc), (3, cc)]
+        extras = {
+            2: [(GR, 0)],
+            3: [(GN, 0)],
+            4: [(GZ, 0), (3, 0)],
+            5: [(GR, 1)],
+            7: [(GZ, 1)],
+            8: [(GN, 1)],
+            9: [(3, 1), (GR, 2)],
+            11: [(GZ, 2)],
+            13: [(GN, 2)],
+            14: [(3, 2)],
+        }
 
         def issue_load(k):
             if k >= n_units:
@@ -349,9 +356,13 @@ def tile_grucellstack_pa_kernel(tc, x, h0, gh0, w, b, out_0, out_1):
         v_add(c)
         act("n", t[("v", c)], ("n", c), ACT.Tanh, CW)
         t[("d", c)] = work("d", CW)
-        nc.gpsimd.tensor_tensor(
-            out=t[("d", c)][:], in0=part(hp[c // 2], c, 0, CW), in1=t[("n", c)][:], op=ALU.subtract
-        )
+        for lo in (0, P):
+            nc.gpsimd.tensor_tensor(
+                out=t[("d", c)][:, :, lo : lo + P],
+                in0=part(hp[c // 2], c, lo, P),
+                in1=t[("n", c)][:, :, lo : lo + P],
+                op=ALU.subtract,
+            )
         quantize(kb, 2)
         acc_m = []
         for m in range(2):

@@ -112,11 +112,8 @@ def tile_grucellstack_pa_kernel(tc, x, h0, gh0, w, b, out_0, out_1):
             halves = []
             if k < HALF_UNITS:
                 for hf in range(2):
-                    r_t = rawp.tile([P, nj, 1024], BF16, name="rawh", tag="rawh", bufs=2 * HALF_UNITS)
-                    nc.sync.dma_start(
-                        out=r_t[:],
-                        in_=src[r0 : r0 + nj * P, hf * 1024 : (hf + 1) * 1024].rearrange("(j p) k -> p j k", p=P),
-                    )
+                    r_t = rawp.tile([P, IN], BF16, name="rawh", tag="rawh", bufs=2 * HALF_UNITS)
+                    nc.sync.dma_start(out=r_t[:], in_=src[r0 + hf * P : r0 + (hf + 1) * P, :])
                     halves.append(r_t)
                     if k == 0 and hf == 0:
                         nc.sync.dma_start(out=btile[0:9, :], in_=b.rearrange("(q n) -> q n", q=9))
@@ -138,17 +135,21 @@ def tile_grucellstack_pa_kernel(tc, x, h0, gh0, w, b, out_0, out_1):
             for bq in range(first, first + count):
                 bank = tps.tile([P, 2, 2, P], F32, name="tp", tag="tp")
                 for s in range(2):
-                    if nj == 2:
-                        g, j = bq, s
+                    if k < HALF_UNITS:
+                        g = 2 * (bq % 2) + s
+                        words = raw[k][bq // 2][:, 512 * g : 512 * (g + 1)].bitcast(F32)
                     else:
-                        g, j = 2 * bq + s, 0
-                    hf, gl = divmod(g, 2)
-                    words = raw[k][hf][:, j, :].bitcast(F32)
+                        if nj == 2:
+                            g, j = bq, s
+                        else:
+                            g, j = 2 * bq + s, 0
+                        words = raw[k][g // 2][:, j, 512 * (g % 2) : 512 * (g % 2 + 1)].bitcast(F32)
                     for u in range(2):
-                        nc.tensor.transpose(
-                            bank[:, s, u, :], words[:, 256 * gl + u : 256 * (gl + 1) : 2], ident_f[:]
-                        )
-                if nj == 2:
+                        nc.tensor.transpose(bank[:, s, u, :], words[:, u:256:2], ident_f[:])
+                if k < HALF_UNITS:
+                    g0, j = 2 * (bq % 2), bq // 2
+                    dst = grouped[k][:, g0 : g0 + 2, j * P : (j + 1) * P, :].bitcast(F32)
+                elif nj == 2:
                     dst = grouped[k][:, bq, :, :].bitcast(F32).rearrange("p (s r) u -> p s r u", s=2)
                 else:
                     dst = grouped[k][:, 2 * bq : 2 * bq + 2, :, :].bitcast(F32)

@@ -116,7 +116,8 @@ def tile_grucellstack_pa_kernel(tc, x, h0, gh0, w, b, out_0, out_1):
                     nc.sync.dma_start(out=r_t[:], in_=src[r0 + hf * P : r0 + (hf + 1) * P, :])
                     halves.append(r_t)
                     if k == 0 and hf == 0:
-                        nc.sync.dma_start(out=btile[0:9, :], in_=b.rearrange("(q n) -> q n", q=9))
+                        nc.sync.dma_start(out=btile[0:8, :], in_=b[0 : 8 * 512].rearrange("(q n) -> q n", q=8))
+                        nc.sync.dma_start(out=btile[8:9, :], in_=b[8 * 512 : 9 * 512].rearrange("(q n) -> q n", q=1))
             else:
                 r_t = rawp.tile([P, nj, IN], BF16, name="rawf", tag="rawf", bufs=RAW_FULL)
                 nc.sync.dma_start(out=r_t[:], in_=src[r0 : r0 + nj * P, :].rearrange("(j p) k -> p j k", p=P))

@@ -49,16 +49,16 @@ def tile_grucellstack_pa_kernel(tc, x, h0, gh0, w, b, out_0, out_1):
                 units.append((w, GZ * L + c * CW + P, 1))
         n_units = len(units)
 
-        btile = const.tile([P, 512], BF16, name="btile")
-        nc.vector.memset(btile[:], 0.0)
         ztile = const.tile([P, 512], BF16, name="ztile")
         nc.vector.memset(ztile[:], 0.0)
         zeros = const.tile([P, 1], F32, name="zeros")
         nc.vector.memset(zeros[:], 0.0)
-        ident_b = const.tile([P, P], BF16, name="ident_b")
-        make_identity(nc, ident_b[:])
         ident_f = const.tile([P, P], F32, name="ident_f")
         make_identity(nc, ident_f[:])
+        bwords = const.tile([P, 4, 16], BF16, name="bwords")
+        nc.scalar.dma_start(out=bwords[:, :, 0:8], in_=b[0:4096].rearrange("(i p t) -> p i t", i=4, p=P))
+        bwords_end = const.tile([P, 4], BF16, name="bwords_end")
+        nc.scalar.dma_start(out=bwords_end[:], in_=b[4096:4608].rearrange("(p t) -> p t", p=P))
         scr = const.tile([P, 1], F32, name="scr")
         nc.scalar.activation(out=scr[:], in_=zeros[:], func=ACT.Sigmoid)
 
@@ -115,9 +115,6 @@ def tile_grucellstack_pa_kernel(tc, x, h0, gh0, w, b, out_0, out_1):
                     r_t = rawp.tile([P, IN], BF16, name="rawh", tag="rawh", bufs=2 * HALF_UNITS)
                     nc.sync.dma_start(out=r_t[:], in_=src[r0 + hf * P : r0 + (hf + 1) * P, :])
                     halves.append(r_t)
-                    if k == 0 and hf == 0:
-                        nc.sync.dma_start(out=btile[0:8, :], in_=b[0 : 8 * 512].rearrange("(q n) -> q n", q=8))
-                        nc.sync.dma_start(out=btile[8:9, :], in_=b[8 * 512 : 9 * 512].rearrange("(q n) -> q n", q=1))
             else:
                 r_t = rawp.tile([P, nj, IN], BF16, name="rawf", tag="rawf", bufs=RAW_FULL)
                 nc.sync.dma_start(out=r_t[:], in_=src[r0 : r0 + nj * P, :].rearrange("(j p) k -> p j k", p=P))
@@ -188,14 +185,22 @@ def tile_grucellstack_pa_kernel(tc, x, h0, gh0, w, b, out_0, out_1):
         def warm_mm(count):
             ps = accs.tile([P, 512], F32, name="wps", tag="acc")
             for rep in range(count):
-                nc.tensor.matmul(out=ps[:], lhsT=ident_b[:], rhs=ztile[:], start=True, stop=True)
+                nc.tensor.matmul(out=ps[:], lhsT=ztile[:, 0:P], rhs=ztile[:], start=True, stop=True)
 
-        def bias_mm(q):
-            ps = accs.tile([P, 512], F32, name="bps", tag="acc")
-            nc.tensor.matmul(
-                out=ps[:], lhsT=ident_b[:, q : q + 1].to_broadcast([P, P]), rhs=btile[:], start=True, stop=True
+        def bias_spread(i):
+            nw = 4 if i < 4 else 2
+            ps = accs.tile([P, nw, P], F32, name="bps", tag="acc")
+            for u in range(nw):
+                if i < 4:
+                    word = bwords[:, i, 2 * u : 2 * u + 2].bitcast(F32)
+                else:
+                    word = bwords_end[:, 2 * u : 2 * u + 2].bitcast(F32)
+                nc.tensor.transpose(ps[:, u, :], word.to_broadcast([P, P]), ident_f[:])
+            lo = 1024 * i
+            nc.vector.tensor_copy(
+                out=bias_bc[:, lo : lo + 256 * nw].bitcast(F32).rearrange("p (r u) -> p r u", u=nw),
+                in_=ps[:].rearrange("p u r -> p r u"),
             )
-            nc.vector.tensor_copy(out=bias_bc[:, 512 * q : 512 * (q + 1)], in_=ps[:])
 
         def work(name, wd):
             return wk.tile([P, 2, wd], F32, name=name, tag=name)
@@ -277,22 +282,16 @@ def tile_grucellstack_pa_kernel(tc, x, h0, gh0, w, b, out_0, out_1):
             if p < n_units:
                 n_banks = 2 * units[p][2]
                 if p == 0:
+                    bias_spread(0)
+                    bias_spread(3)
                     transposes(p, 0, 2)
-                    bias_mm(0)
-                    bias_mm(3)
+                    bias_spread(1)
                     transposes(p, 2, 2)
-                    bias_mm(6)
-                    bias_mm(1)
+                    bias_spread(2)
                 else:
                     transposes(p, 0, n_banks)
                 if p == 1:
-                    bias_mm(4)
-                    bias_mm(7)
-                if p == 2:
-                    bias_mm(2)
-                    bias_mm(5)
-                if p == 3:
-                    bias_mm(8)
+                    bias_spread(4)
                 if p >= HALF_UNITS:
                     issue_load(p + RAW_FULL)
             if p >= 2:

@@ -22,6 +22,7 @@ NCH = L // CW
 HALF_UNITS = 3
 RAW_FULL = 6
 STORE_FROM = 3
+KEEP = 192
 SPLIT = 640
 GR, GZ, GN = 0, 1, 2
 
@@ -132,6 +133,14 @@ def tile_grucellstack_pa_kernel(tc, x, h0, gh0, w, b, out_0, out_1):
                 grouped[k] = grp.tile([P, 4, nj * P, 4], BF16, name="grouped", tag="grouped", align_bytes=64)
             for bq in range(first, first + count):
                 bank = tps.tile([P, 2, 2, P], F32, name="tp", tag="tp")
+                if bq == 2:
+                    nc.tensor.matmul(
+                        out=bank[:].rearrange("p s u r -> p (s u r)")[:, 0:KEEP],
+                        lhsT=ztile[:, 0:P],
+                        rhs=ztile[:, 0:KEEP],
+                        start=True,
+                        stop=True,
+                    )
                 for s in range(2):
                     if k < HALF_UNITS:
                         g = 2 * (bq % 2) + s

@@ -132,10 +132,10 @@ def tile_grucellstack_pa_kernel(tc, x, h0, gh0, w, b, out_0, out_1):
             if first == 0:
                 grouped[k] = grp.tile([P, 4, nj * P, 4], BF16, name="grouped", tag="grouped", align_bytes=64)
             for bq in range(first, first + count):
-                bank = tps.tile([P, 2, 2, P], F32, name="tp", tag="tp")
+                bank = tps.tile([P, 2, 2 * P], F32, name="tp", tag="tp")
                 if bq == 2:
                     nc.tensor.matmul(
-                        out=bank[:].rearrange("p s u r -> p (s u r)")[:, 0:KEEP],
+                        out=bank[:].rearrange("p u n -> p (u n)")[:, 0:KEEP],
                         lhsT=ztile[:, 0:P],
                         rhs=ztile[:, 0:KEEP],
                         start=True,
@@ -152,15 +152,20 @@ def tile_grucellstack_pa_kernel(tc, x, h0, gh0, w, b, out_0, out_1):
                             g, j = 2 * bq + s, 0
                         words = raw[k][g // 2][:, j, 512 * (g % 2) : 512 * (g % 2 + 1)].bitcast(F32)
                     for u in range(2):
-                        nc.tensor.transpose(bank[:, s, u, :], words[:, u:256:2], ident_f[:])
+                        nc.tensor.transpose(bank[:, u, s * P : (s + 1) * P], words[:, u:256:2], ident_f[:])
                 if k < HALF_UNITS:
                     g0, j = 2 * (bq % 2), bq // 2
                     dst = grouped[k][:, g0 : g0 + 2, j * P : (j + 1) * P, :].bitcast(F32)
-                elif nj == 2:
-                    dst = grouped[k][:, bq, :, :].bitcast(F32).rearrange("p (s r) u -> p s r u", s=2)
+                    nc.scalar.copy(out=dst, in_=bank[:].rearrange("p u (s r) -> p s r u", s=2))
                 else:
-                    dst = grouped[k][:, 2 * bq : 2 * bq + 2, :, :].bitcast(F32)
-                nc.scalar.copy(out=dst, in_=bank[:].rearrange("p s u r -> p s r u"))
+                    if nj == 2:
+                        dst = grouped[k][:, bq, :, :].bitcast(F32)
+                    else:
+                        dst = grouped[k][:, 2 * bq : 2 * bq + 2, :, :].rearrange("p g r t -> p (g r) t").bitcast(F32)
+                    nc.scalar.copy(
+                        out=dst.rearrange("p (c i) u -> p c u i", i=2),
+                        in_=bank[:].rearrange("p u (c i) -> p c u i", i=2),
+                    )
 
         def quantize(k, parts=1):
             nj = units[k][2]

@@ -34,6 +34,7 @@ def tile_grucellstack_pa_kernel(tc, x, h0, gh0, w, b, out_0, out_1):
         rawp = ctx.enter_context(tc.tile_pool(name="rawp", bufs=RAW_FULL))
         grp = ctx.enter_context(tc.tile_pool(name="grp", bufs=3))
         cdp = ctx.enter_context(tc.tile_pool(name="cdp", bufs=3))
+        spl = ctx.enter_context(tc.tile_pool(name="spl", bufs=2))
         wk = ctx.enter_context(tc.tile_pool(name="wk", bufs=2))
         tps = ctx.enter_context(tc.psum_pool(name="tps", bufs=5))
         accs = ctx.enter_context(tc.psum_pool(name="accs", bufs=3))
@@ -127,6 +128,15 @@ def tile_grucellstack_pa_kernel(tc, x, h0, gh0, w, b, out_0, out_1):
                 else:
                     load_gh(gate, cc)
 
+        split = {}
+
+        def split_words(k):
+            split[k] = spl.tile([P, 2, 2, P], F32, name="split", tag="split")
+            nc.scalar.copy(
+                out=split[k][:],
+                in_=raw[k][1][:, :, 512:1024].bitcast(F32).rearrange("p j (n u) -> p j u n", u=2),
+            )
+
         def transposes(k, first, count):
             nj = units[k][2]
             if first == 0:
@@ -152,7 +162,11 @@ def tile_grucellstack_pa_kernel(tc, x, h0, gh0, w, b, out_0, out_1):
                             g, j = 2 * bq + s, 0
                         words = raw[k][g // 2][:, j, 512 * (g % 2) : 512 * (g % 2 + 1)].bitcast(F32)
                     for u in range(2):
-                        nc.tensor.transpose(bank[:, u, s * P : (s + 1) * P], words[:, u:256:2], ident_f[:])
+                        if bq == 3 and k in split:
+                            piece = split[k][:, s, u, :]
+                        else:
+                            piece = words[:, u:256:2]
+                        nc.tensor.transpose(bank[:, u, s * P : (s + 1) * P], piece, ident_f[:])
                 if k < HALF_UNITS:
                     g0, j = 2 * (bq % 2), bq // 2
                     dst = grouped[k][:, g0 : g0 + 2, j * P : (j + 1) * P, :].bitcast(F32)
@@ -289,7 +303,7 @@ def tile_grucellstack_pa_kernel(tc, x, h0, gh0, w, b, out_0, out_1):
         for k in range(HALF_UNITS + RAW_FULL):
             issue_load(k)
         warm_mm(3)
-        early_gsum = {2: (GR, 0), 3: (GZ, 0), 5: (GR, 1), 8: (GZ, 1), 11: (GR, 2), 14: (GZ, 2)}
+        early_gsum = {2: (GR, 0), 4: (GZ, 0), 5: (GR, 1), 8: (GZ, 1), 11: (GR, 2), 14: (GZ, 2)}
         last = NCH - 1
 
         for p in range(n_units - 3):
@@ -339,8 +353,10 @@ def tile_grucellstack_pa_kernel(tc, x, h0, gh0, w, b, out_0, out_1):
                         amax_chunk(c - 1, 1)
             if p in early_gsum:
                 g_sum(early_gsum[p][0], early_gsum[p][1])
+            if p + 1 >= HALF_UNITS and p % 3 != 1:
+                split_words(p + 1)
             if p < n_units - 1:
-                quantize(p)
+                quantize(p, 2)
 
         c = last
         k0 = 1 + 3 * c
@@ -405,10 +421,11 @@ def tile_grucellstack_pa_kernel(tc, x, h0, gh0, w, b, out_0, out_1):
         e_mul(c, 0, P)
         t[("e", c, P)] = work("e", P)
         cols = slice(L - P, L)
-        for m in range(2):
-            tt(t[("e", c, P)][:, m, :], t[("z", c, P)][:, m, :], t[("d", c)][:, m, P:CW], ALU.mult)
         tt(o_all[:, :, L - CW : L - P], t[("n", c)][:, :, 0:P], t[("e", c, 0)][:], ALU.add)
         for m in range(2):
+            tt(t[("e", c, P)][:, m, :], t[("z", c, P)][:, m, :], t[("d", c)][:, m, P:CW], ALU.mult)
+        for m in range(2):
+            amax(o_all[:, m, L + 1 : L + 2], m, L - CW, L - P)
             tt(o_all[:, m, cols], t[("n", c)][:, m, P:CW], t[("e", c, P)][:, m, :], ALU.add)
         cols = slice(L - CW, L)
         nc.sync.dma_start(out=out_0[:, cols].rearrange("(m p) n -> p m n", p=P), in_=o_all[:, :, cols])
@@ -417,7 +434,7 @@ def tile_grucellstack_pa_kernel(tc, x, h0, gh0, w, b, out_0, out_1):
         rcp = const.tile([P, 2], F32, name="rcp")
         fac = const.tile([P, 2], F32, name="fac")
         for m in (0, 1):
-            amax(amx[:, m : m + 1], m, L - CW, L + 1)
+            amax(amx[:, m : m + 1], m, L - P, L + 2)
         for m in (0, 1):
             nc.vector.reciprocal(out=rcp[:, m : m + 1], in_=amx[:, m : m + 1])
         for m in (0, 1):

from contextlib import ExitStack

import concourse.mybir as mybir
from concourse.masks import make_identity

F32 = mybir.dt.float32
BF16 = mybir.dt.bfloat16
U32 = mybir.dt.uint32
U8 = mybir.dt.uint8
FP8X4 = mybir.dt.float8_e4m3fn_x4
FP8 = mybir.dt.float8_e4m3fn
ALU = mybir.AluOpType
ACT = mybir.ActivationFunctionType
AX = mybir.AxisListType

B, IN, L = 256, 2048, 1536
FLOPS = 2 * B * IN * 3 * L

P = 128
CW = 256
NCH = L // CW
HALF_UNITS = 3
RAW_FULL = 6
STORE_FROM = 3
KEEP = 192
SPLIT = 640
GR, GZ, GN = 0, 1, 2


def tile_grucellstack_pa_kernel(tc, x, h0, gh0, w, b, out_0, out_1):
    nc = tc.nc
    with ExitStack() as ctx:
        const = ctx.enter_context(tc.tile_pool(name="const", bufs=1))
        rawp = ctx.enter_context(tc.tile_pool(name="rawp", bufs=RAW_FULL))
        grp = ctx.enter_context(tc.tile_pool(name="grp", bufs=3))
        cdp = ctx.enter_context(tc.tile_pool(name="cdp", bufs=3))
        spl = ctx.enter_context(tc.tile_pool(name="spl", bufs=2))
        wk = ctx.enter_context(tc.tile_pool(name="wk", bufs=2))
        tps = ctx.enter_context(tc.psum_pool(name="tps", bufs=5))
        accs = ctx.enter_context(tc.psum_pool(name="accs", bufs=3))
        ctx.enter_context(tc.manual_schedule())

        units = [(x, 0, 2)]
        for c in range(NCH):
            units.append((w, GR * L + c * CW, 2))
            units.append((w, GN * L + c * CW, 2))
            if c < NCH - 1:
                units.append((w, GZ * L + c * CW, 2))
            else:
                units.append((w, GZ * L + c * CW, 1))
                units.append((w, GZ * L + c * CW + P, 1))
        n_units = len(units)

        ztile = const.tile([P, 512], BF16, name="ztile")
        nc.vector.memset(ztile[:], 0.0)
        zeros = const.tile([P, 1], F32, name="zeros")
        nc.vector.memset(zeros[:], 0.0)
        ident_f = const.tile([P, P], F32, name="ident_f")
        make_identity(nc, ident_f[:])
        bwords = const.tile([P, 4, 16], BF16, name="bwords")
        nc.scalar.dma_start(out=bwords[:, :, 0:8], in_=b[0:4096].rearrange("(i p t) -> p i t", i=4, p=P))
        bwords_end = const.tile([P, 4], BF16, name="bwords_end")
        nc.scalar.dma_start(out=bwords_end[:], in_=b[4096:4608].rearrange("(p t) -> p t", p=P))
        scr = const.tile([P, 1], F32, name="scr")
        nc.scalar.activation(out=scr[:], in_=zeros[:], func=ACT.Sigmoid)

        bias_bc = const.tile([P, 3 * L], BF16, name="bias_bc")
        xcodes = const.tile([P, 4, CW], U32, name="xcodes", align_bytes=64)
        xscales = const.tile([P, 4, CW], U8, name="xscales", align_bytes=64)
        o_all = const.tile([P, 2, L + 8], F32, name="o_all")
        q_all = const.tile([P, 2, L], FP8, name="q_all")
        stats = const.tile([P, 2, 8], F32, name="stats")

        raw = {}
        grouped = {}
        codes = {0: xcodes}
        scales = {0: xscales}
        acc = {}
        ghp = {}
        hp = {}
        gsum = {}
        t = {}

        def load_gh(gate, cc):
            g_t = const.tile([P, 2, 512], BF16, name="gh%d_%d" % (gate, cc))
            lo = gate * L + cc * 512
            nc.sync.dma_start(out=g_t[:], in_=gh0[:, lo : lo + 512].rearrange("(m p) n -> p m n", p=P))
            ghp[(gate, cc)] = g_t

        def load_h(cc):
            h_t = const.tile([P, 2, 512], BF16, name="h_%d" % cc)
            nc.sync.dma_start(
                out=h_t[:], in_=h0[:, cc * 512 : (cc + 1) * 512].rearrange("(m p) n -> p m n", p=P)
            )
            hp[cc] = h_t

        extras = {
            2: [(GR, 0)],
            3: [(GN, 0)],
            4: [(GZ, 0), (3, 0)],
            5: [(GR, 1)],
            7: [(GZ, 1)],
            8: [(GN, 1)],
            9: [(3, 1), (GR, 2)],
            11: [(GZ, 2)],
            13: [(GN, 2)],
            14: [(3, 2)],
        }

        def issue_load(k):
            if k >= n_units:
                return
            src, r0, nj = units[k]
            halves = []
            if k < HALF_UNITS:
                for hf in range(2):
                    r_t = rawp.tile([P, IN], BF16, name="rawh", tag="rawh", bufs=2 * HALF_UNITS)
                    nc.sync.dma_start(out=r_t[:], in_=src[r0 + hf * P : r0 + (hf + 1) * P, :])
                    halves.append(r_t)
            else:
                r_t = rawp.tile([P, nj, IN], BF16, name="rawf", tag="rawf", bufs=RAW_FULL)
                nc.sync.dma_start(out=r_t[:], in_=src[r0 : r0 + nj * P, :].rearrange("(j p) k -> p j k", p=P))
                halves = [r_t[:, :, 0:1024], r_t[:, :, 1024:IN]]
            raw[k] = halves
            for gate, cc in extras.get(k, []):
                if gate == 3:
                    load_h(cc)
                else:
                    load_gh(gate, cc)

        split = {}

        def split_words(k):
            split[k] = spl.tile([P, 2, 2, P], F32, name="split", tag="split")
            nc.scalar.copy(
                out=split[k][:],
                in_=raw[k][1][:, :, 512:1024].bitcast(F32).rearrange("p j (n u) -> p j u n", u=2),
            )

        def transposes(k, first, count):
            nj = units[k][2]
            if first == 0:
                grouped[k] = grp.tile([P, 4, nj * P, 4], BF16, name="grouped", tag="grouped", align_bytes=64)
            for bq in range(first, first + count):
                bank = tps.tile([P, 2, 2 * P], F32, name="tp", tag="tp")
                if bq == 2:
                    nc.tensor.matmul(
                        out=bank[:].rearrange("p u n -> p (u n)")[:, 0:KEEP],
                        lhsT=ztile[:, 0:P],
                        rhs=ztile[:, 0:KEEP],
                        start=True,
                        stop=True,
                    )
                for s in range(2):
                    if k < HALF_UNITS:
                        g = 2 * (bq % 2) + s
                        words = raw[k][bq // 2][:, 512 * g : 512 * (g + 1)].bitcast(F32)
                    else:
                        if nj == 2:
                            g, j = bq, s
                        else:
                            g, j = 2 * bq + s, 0
                        words = raw[k][g // 2][:, j, 512 * (g % 2) : 512 * (g % 2 + 1)].bitcast(F32)
                    for u in range(2):
                        if bq == 3 and k in split:
                            piece = split[k][:, s, u, :]
                        else:
                            piece = words[:, u:256:2]
                        nc.tensor.transpose(bank[:, u, s * P : (s + 1) * P], piece, ident_f[:])
                if k < HALF_UNITS:
                    g0, j = 2 * (bq % 2), bq // 2
                    dst = grouped[k][:, g0 : g0 + 2, j * P : (j + 1) * P, :].bitcast(F32)
                    nc.scalar.copy(out=dst, in_=bank[:].rearrange("p u (s r) -> p s r u", s=2))
                else:
                    if nj == 2:
                        dst = grouped[k][:, bq, :, :].bitcast(F32)
                    else:
                        dst = grouped[k][:, 2 * bq : 2 * bq + 2, :, :].rearrange("p g r t -> p (g r) t").bitcast(F32)
                    nc.scalar.copy(
                        out=dst.rearrange("p (c i) u -> p c u i", i=2),
                        in_=bank[:].rearrange("p u (c i) -> p c u i", i=2),
                    )

        def quantize(k, parts=1):
            nj = units[k][2]
            if k > 0:
                codes[k] = cdp.tile([P, 4, nj * P], U32, name="wc", tag="wc", align_bytes=64)
                scales[k] = cdp.tile([P, 4, nj * P], U8, name="ws", tag="ws", align_bytes=64)
            ng = 4 // parts
            for g0 in range(0, 4, ng):
                nc.vector.quantize_mx(
                    out=codes[k][:, g0 : g0 + ng, :].rearrange("p g c -> p (g c)").bitcast(FP8X4),
                    scales=scales[k][:, g0 : g0 + ng, :].rearrange("p g c -> p (g c)"),
                    in_=grouped[k][:, g0 : g0 + ng, :, :].rearrange("p g c t -> p (g c t)"),
                )

        def matmuls(k):
            nj = units[k][2]
            a_t = accs.tile([P, 2, nj * P], F32, name="acc", tag="acc")
            for m in range(2):
                for g in range(4):
                    nc.tensor.matmul_mx(
                        out=a_t[:, m, :],
                        lhsT=xcodes[:, g, m * P : (m + 1) * P].bitcast(FP8X4),
                        lhsT_scale=xscales[:, g, m * P : (m + 1) * P],
                        rhs=codes[k][:, g, :].bitcast(FP8X4),
                        rhs_scale=scales[k][:, g, :],
                        start=(g == 0),
                        stop=(g == 3),
                    )
            acc[k] = a_t

        def warm_mm(count):
            ps = accs.tile([P, 512], F32, name="wps", tag="acc")
            for rep in range(count):
                nc.tensor.matmul(out=ps[:], lhsT=ztile[:, 0:P], rhs=ztile[:], start=True, stop=True)

        def bias_spread(i):
            nw = 4 if i < 4 else 2
            ps = accs.tile([P, nw, P], F32, name="bps", tag="acc")
            for u in range(nw):
                if i < 4:
                    word = bwords[:, i, 2 * u : 2 * u + 2].bitcast(F32)
                else:
                    word = bwords_end[:, 2 * u : 2 * u + 2].bitcast(F32)
                nc.tensor.transpose(ps[:, u, :], word.to_broadcast([P, P]), ident_f[:])
            lo = 1024 * i
            nc.vector.tensor_copy(
                out=bias_bc[:, lo : lo + 256 * nw].bitcast(F32).rearrange("p (r u) -> p r u", u=nw),
                in_=ps[:].rearrange("p u r -> p r u"),
            )

        def work(name, wd):
            return wk.tile([P, 2, wd], F32, name=name, tag=name)

        def tt(out, in0, in1, op):
            nc.vector.tensor_tensor(out=out, in0=in0, in1=in1, op=op)

        def part(tile_ap, c, lo, wd):
            off = (c % 2) * CW + lo
            return tile_ap[:, :, off : off + wd]

        def g_sum(gate, cc):
            gsum[(gate, cc)] = const.tile([P, 2, 512], F32, name="gs%d_%d" % (gate, cc))
            lo = gate * L + cc * 512
            tt(
                gsum[(gate, cc)][:],
                ghp[(gate, cc)][:],
                bias_bc[:, lo : lo + 512].unsqueeze(1).to_broadcast([P, 2, 512]),
                ALU.add,
            )

        def a_rz(gate, k, c, lo, wd):
            t[("A", gate, c, lo)] = work("A%d" % gate, wd)
            tt(t[("A", gate, c, lo)][:], acc[k][:], part(gsum[(gate, c // 2)], c, lo, wd), ALU.add)

        def act(dst, src, key, func, wd):
            t[key] = src
            nc.scalar.activation(out=src[:], in_=src[:], func=func)

        def a_n(k, c):
            t[("A", GN, c)] = work("A2", CW)
            lo = GN * L + c * CW
            tt(
                t[("A", GN, c)][:],
                acc[k][:],
                bias_bc[:, lo : lo + CW].unsqueeze(1).to_broadcast([P, 2, CW]),
                ALU.add,
            )

        def u_mul(c):
            t[("u", c)] = work("u", CW)
            tt(t[("u", c)][:], t[("r", c)][:], part(ghp[(GN, c // 2)], c, 0, CW), ALU.mult)

        def v_add(c):
            t[("v", c)] = work("v", CW)
            tt(t[("v", c)][:], t[("A", GN, c)][:], t[("u", c)][:], ALU.add)

        def d_sub(c):
            t[("d", c)] = work("d", CW)
            tt(t[("d", c)][:], part(hp[c // 2], c, 0, CW), t[("n", c)][:], ALU.subtract)

        def e_mul(c, lo, wd):
            t[("e", c, lo)] = work("e", wd)
            tt(t[("e", c, lo)][:], t[("z", c, lo)][:], t[("d", c)][:, :, lo : lo + wd], ALU.mult)

        def o_add(c, lo, wd):
            cols = slice(c * CW + lo, c * CW + lo + wd)
            tt(o_all[:, :, cols], t[("n", c)][:, :, lo : lo + wd], t[("e", c, lo)][:], ALU.add)
            if c == STORE_FROM:
                cols = slice(0, (c + 1) * CW)
            if c >= STORE_FROM:
                nc.sync.dma_start(out=out_0[:, cols].rearrange("(m p) n -> p m n", p=P), in_=o_all[:, :, cols])

        def amax(dst, m, lo, hi):
            nc.vector.tensor_reduce(
                out=dst, in_=o_all[:, m, lo:hi], axis=AX.X, op=ALU.max, apply_absolute_value=True
            )

        def amax_chunk(c, m):
            amax(stats[:, m, c : c + 1], m, c * CW, (c + 1) * CW)

        for k in range(HALF_UNITS + RAW_FULL):
            issue_load(k)
        warm_mm(3)
        early_gsum = {2: (GR, 0), 4: (GZ, 0), 5: (GR, 1), 8: (GZ, 1), 11: (GR, 2), 14: (GZ, 2)}
        last = NCH - 1

        for p in range(n_units - 3):
            if p < n_units:
                n_banks = 2 * units[p][2]
                if p == 0:
                    bias_spread(0)
                    bias_spread(3)
                    transposes(p, 0, 2)
                    bias_spread(1)
                    transposes(p, 2, 2)
                    bias_spread(2)
                else:
                    transposes(p, 0, n_banks)
                if p == 1:
                    bias_spread(4)
                if p >= HALF_UNITS:
                    issue_load(p + RAW_FULL)
            if p >= 2:
                matmuls(p - 1)
            if p >= 3:
                c, ph = divmod(p - 3, 3)
                k0 = 1 + 3 * c
                if ph == 0:
                    if c >= 1:
                        e_mul(c - 1, 0, CW)
                    a_rz(GR, k0, c, 0, CW)
                    if c >= 1:
                        o_add(c - 1, 0, CW)
                    act("r", t[("A", GR, c, 0)], ("r", c), ACT.Sigmoid, CW)
                elif ph == 1:
                    a_n(k0 + 1, c)
                    u_mul(c)
                    if c == last:
                        amax_chunk(c - 1, 0)
                        amax_chunk(c - 1, 1)
                        quantize(p, 2)
                    elif c >= 1:
                        amax_chunk(c - 1, 0)
                    v_add(c)
                    act("n", t[("v", c)], ("n", c), ACT.Tanh, CW)
                elif c < last:
                    d_sub(c)
                    a_rz(GZ, k0 + 2, c, 0, CW)
                    act("z", t[("A", GZ, c, 0)], ("z", c, 0), ACT.Sigmoid, CW)
                    if c >= 1:
                        amax_chunk(c - 1, 1)
            if p in early_gsum:
                g_sum(early_gsum[p][0], early_gsum[p][1])
            if p + 1 >= HALF_UNITS and p % 3 != 1:
                split_words(p + 1)
            if p < n_units - 1:
                quantize(p, 2)

        c = last
        k0 = 1 + 3 * c
        ka, kb = k0 + 2, k0 + 3
        transposes(k0 + 1, 0, 4)
        matmuls(k0)
        d_sub(c - 1)
        a_rz(GZ, k0 - 1, c - 1, 0, CW)
        act("z", t[("A", GZ, c - 1, 0)], ("z", c - 1, 0), ACT.Sigmoid, CW)
        amax_chunk(c - 2, 1)
        quantize(k0 + 1, 2)
        a_rz(GR, k0, c, 0, CW)
        act("r", t[("A", GR, c, 0)], ("r", c), ACT.Sigmoid, CW)
        transposes(ka, 0, 2)
        matmuls(k0 + 1)
        t[("e", c - 1, 0)] = work("e", CW)
        cols = slice((c - 1) * CW, c * CW)
        for m in range(2):
            tt(t[("e", c - 1, 0)][:, m, :], t[("z", c - 1, 0)][:, m, :], t[("d", c - 1)][:, m, :], ALU.mult)
        for m in range(2):
            tt(o_all[:, m, cols], t[("n", c - 1)][:, m, :], t[("e", c - 1, 0)][:, m, :], ALU.add)
        nc.sync.dma_start(out=out_0[:, cols].rearrange("(m p) n -> p m n", p=P), in_=o_all[:, :, cols])
        u_mul(c)
        transposes(kb, 0, 2)
        a_n(k0 + 1, c)
        quantize(ka)
        matmuls(ka)
        v_add(c)
        act("n", t[("v", c)], ("n", c), ACT.Tanh, CW)
        t[("d", c)] = work("d", CW)
        for lo in (0, P):
            nc.gpsimd.tensor_tensor(
                out=t[("d", c)][:, :, lo : lo + P],
                in0=part(hp[c // 2], c, lo, P),
                in1=t[("n", c)][:, :, lo : lo + P],
                op=ALU.subtract,
            )
        quantize(kb, 2)
        acc_m = []
        for m in range(2):
            acc_m.append(accs.tile([P, P], F32, name="accm", tag="acc"))
        for g in range(4):
            for m in range(2):
                nc.tensor.matmul_mx(
                    out=acc_m[m][:],
                    lhsT=xcodes[:, g, m * P : (m + 1) * P].bitcast(FP8X4),
                    lhsT_scale=xscales[:, g, m * P : (m + 1) * P],
                    rhs=codes[kb][:, g, :].bitcast(FP8X4),
                    rhs_scale=scales[kb][:, g, :],
                    start=(g == 0),
                    stop=(g == 3),
                )
        a_rz(GZ, ka, c, 0, P)
        act("z", t[("A", GZ, c, 0)], ("z", c, 0), ACT.Sigmoid, P)
        amax_chunk(c - 1, 0)
        amax_chunk(c - 1, 1)
        t[("A", GZ, c, P)] = work("A1", P)
        for m in range(2):
            tt(t[("A", GZ, c, P)][:, m, :], acc_m[m][:], part(gsum[(GZ, c // 2)], c, P, P)[:, m, :], ALU.add)
        act("z", t[("A", GZ, c, P)], ("z", c, P), ACT.Sigmoid, P)
        nc.vector.tensor_reduce(out=o_all[:, :, L : L + 1], in_=stats[:, :, 0:last], axis=AX.X, op=ALU.max)
        e_mul(c, 0, P)
        t[("e", c, P)] = work("e", P)
        cols = slice(L - P, L)
        tt(o_all[:, :, L - CW : L - P], t[("n", c)][:, :, 0:P], t[("e", c, 0)][:], ALU.add)
        for m in range(2):
            tt(t[("e", c, P)][:, m, :], t[("z", c, P)][:, m, :], t[("d", c)][:, m, P:CW], ALU.mult)
        for m in range(2):
            amax(o_all[:, m, L + 1 : L + 2], m, L - CW, L - P)
            tt(o_all[:, m, cols], t[("n", c)][:, m, P:CW], t[("e", c, P)][:, m, :], ALU.add)
        cols = slice(L - CW, L)
        nc.sync.dma_start(out=out_0[:, cols].rearrange("(m p) n -> p m n", p=P), in_=o_all[:, :, cols])

        amx = const.tile([P, 2], F32, name="amx")
        rcp = const.tile([P, 2], F32, name="rcp")
        fac = const.tile([P, 2], F32, name="fac")
        for m in (0, 1):
            amax(amx[:, m : m + 1], m, L - P, L + 2)
        for m in (0, 1):
            nc.vector.reciprocal(out=rcp[:, m : m + 1], in_=amx[:, m : m + 1])
        for m in (0, 1):
            nc.vector.tensor_scalar(
                out=fac[:, m : m + 1], in0=rcp[:, m : m + 1], scalar1=448.0, scalar2=None, op0=ALU.mult
            )
        nc.scalar.activation(
            out=q_all[:, 1, SPLIT:L],
            in_=o_all[:, 1, SPLIT:L],
            func=ACT.Identity,
            scale=fac[:, 1:2],
            bias=zeros[:, 0:1],
            saturate=False,
        )
        nc.vector.tensor_scalar(
            out=q_all[:, 0, :], in0=o_all[:, 0, 0:L], scalar1=fac[:, 0:1], scalar2=None, op0=ALU.mult, saturate=False
        )
        nc.sync.dma_start(out=out_1[0:P, :], in_=q_all[:, 0, :].bitcast(U8))
        nc.sync.dma_start(out=out_1[P : 2 * P, SPLIT:L], in_=q_all[:, 1, SPLIT:L].bitcast(U8))
        nc.vector.tensor_scalar(
            out=q_all[:, 1, 0:SPLIT],
            in0=o_all[:, 1, 0:SPLIT],
            scalar1=fac[:, 1:2],
            scalar2=None,
            op0=ALU.mult,
            saturate=False,
        )
        nc.sync.dma_start(out=out_1[P : 2 * P, 0:SPLIT], in_=q_all[:, 1, 0:SPLIT].bitcast(U8))
